import numpy as np
import ml_dtypes


def mxq(x, axis, fmt="e4m3"):
    dtype, down = {"e4m3": (ml_dtypes.float8_e4m3fn, 7), "e5m2": (ml_dtypes.float8_e5m2, 14)}[fmt]
    v = np.moveaxis(np.asarray(x, np.float32).astype(ml_dtypes.bfloat16).astype(np.float64), axis, -1)
    blocks = v.reshape(v.shape[:-1] + (-1, 32))
    amax = np.abs(blocks).max(-1, keepdims=True)
    byte = np.maximum(np.where(amax > 0, np.frexp(amax)[1] - 1 + 127, 0) - down, 1)
    scale = np.exp2(byte - 127.0)
    codes = (blocks / scale).astype(np.float32).astype(dtype).astype(np.float64)
    return np.moveaxis((codes * scale).reshape(v.shape), -1, axis)


WIDE = False


def mx_kscale(k):
    if not WIDE:
        return np.ones(k)
    levels = np.array([10, -10, 5, -5, 0])
    a = np.random.permutation(np.resize(levels, k // 512 * 4)).reshape(k // 512, 4)
    idx = np.arange(k)
    return np.exp2(a[idx // 512, idx % 128 // 32])


BF16 = ml_dtypes.bfloat16


def bf(x):
    return np.asarray(x, np.float32).astype(BF16)


def f64(x):
    return np.asarray(x).astype(np.float64)


B, D0, D1, D2, D3, D4 = 128, 512, 1024, 512, 1024, 256
DENSITY = 0.02


def setup_inputs():
    s, t = mx_kscale(D0), mx_kscale(D1)
    bound0 = np.sqrt(3.0 / (DENSITY * D0))
    bound1 = np.sqrt(6.0 / (DENSITY * D1))
    return {"x": bf(np.random.standard_normal((B, D0)) * s),
            "W0": bf(np.random.uniform(-bound0, bound0, (D1, D0)) / s[None, :] * t[:, None]),
            "b0": bf(np.random.standard_normal(D1) * 0.3 * t),
            "m0": bf(np.random.uniform(size=(D1, D0)) < DENSITY),
            "W1": bf(np.random.uniform(-bound1, bound1, (D2, D1)) / t[None, :]),
            "b1": bf(np.random.standard_normal(D2) * 0.3),
            "m1": bf(np.random.uniform(size=(D2, D1)) < DENSITY)}


def reference(x, W0, b0, m0, W1, b1, m1):
    h = f64(x).reshape(x.shape[0], -1)
    w0 = f64(W0) * f64(m0)
    pre0 = (mxq(h, 1, "e4m3") @ mxq(w0, 1, "e4m3").T) + f64(b0)
    h0 = np.maximum(pre0, 0.0)
    w1 = f64(W1) * f64(m1)
    pre1 = (mxq(h0, 1, "e4m3") @ mxq(w1, 1, "e4m3").T) + f64(b1)
    return np.maximum(pre1, 0.0)

@@ -1,0 +1,177 @@
+from contextlib import ExitStack
+
+import concourse.mybir as mybir
+from concourse.masks import make_identity
+
+BF16 = mybir.dt.bfloat16
+F32 = mybir.dt.float32
+U32 = mybir.dt.uint32
+U8 = mybir.dt.uint8
+FP8X4 = mybir.dt.float8_e4m3fn_x4
+RELU = mybir.ActivationFunctionType.Relu
+
+P = 128
+PACK = 4
+K_PASS = P * PACK
+HALVES = 2
+D0, D1, D2 = 512, 1024, 512
+FLOPS = 2 * P * (D0 * D1 + D1 * D2)
+
+SETS = 2
+CHUNK = SETS * K_PASS
+CHUNKS_0 = D1 * D0 // (P * CHUNK)
+CHUNKS_1 = D2 * D1 // (P * CHUNK)
+CHUNKS = CHUNKS_0 + CHUNKS_1
+PASSES_1 = D1 // K_PASS
+
+
+def tile_patchedsparsenetwork_pa_s_kernel(tc, x, W0, b0, m0, W1, b1, m1, out):
+    nc = tc.nc
+    with ExitStack() as ctx:
+        consts = ctx.enter_context(tc.tile_pool(name="consts", bufs=1))
+        keep = ctx.enter_context(tc.tile_pool(name="keep", bufs=1))
+        stream = ctx.enter_context(tc.tile_pool(name="stream", bufs=CHUNKS))
+        flip_psum = ctx.enter_context(tc.psum_pool(name="flip_psum", bufs=4))
+        h_psum = ctx.enter_context(tc.psum_pool(name="h_psum", bufs=2))
+        out_psum = ctx.enter_context(tc.psum_pool(name="out_psum", bufs=2))
+
+        x_rows = consts.tile([P, D0], BF16)
+        nc.sync.dma_start(out=x_rows[:], in_=x)
+        w_views = [W0.rearrange("(c q e) k -> c q (e k)", q=P, e=SETS)[c] for c in range(CHUNKS_0)]
+        m_views = [m0.rearrange("(c q e) k -> c q (e k)", q=P, e=SETS)[c] for c in range(CHUNKS_0)]
+        w_views += [W1.rearrange("(r q) k -> r q k", q=P)[r] for r in range(CHUNKS_1)]
+        m_views += [m1.rearrange("(r q) k -> r q k", q=P)[r] for r in range(CHUNKS_1)]
+        w_rows, m_rows = [], []
+        for c in range(CHUNKS):
+            w_rows.append(stream.tile([P, CHUNK], BF16, name="w_rows"))
+            nc.sync.dma_start(out=w_rows[c][:], in_=w_views[c])
+            m_rows.append(stream.tile([P, CHUNK], BF16, name="m_rows"))
+            nc.sync.dma_start(out=m_rows[c][:], in_=m_views[c])
+
+        ident = consts.tile([P, P], F32)
+        make_identity(nc, ident[:])
+        ones = consts.tile([P, P], BF16)
+        nc.vector.memset(ones[:], 1.0)
+
+        b1_rows = consts.tile([P, D2], BF16)
+        nc.vector.memset(b1_rows[:], 0.0)
+        nc.scalar.dma_start(out=b1_rows[0:1, :], in_=b1.rearrange("(o n) -> o n", o=1))
+        b1_bank = flip_psum.tile([P, D2], F32, tag="bank")
+        nc.tensor.matmul(out=b1_bank[:], lhsT=ones[:], rhs=b1_rows[:], start=True, stop=True)
+        b1_all = consts.tile([P, D2], F32)
+        nc.scalar.copy(out=b1_all[:], in_=b1_bank[:])
+
+        b0_rows = consts.tile([P, HALVES * P], BF16)
+        nc.vector.memset(b0_rows[:], 0.0)
+        nc.scalar.dma_start(
+            out=b0_rows[0:CHUNKS_0, :], in_=b0.rearrange("(j n) -> j n", j=CHUNKS_0)
+        )
+        b0_bank = flip_psum.tile([P, D2], F32, tag="bank")
+        nc.tensor.transpose(out=b0_bank[:, 0:P], in_=b0_rows[:].bitcast(F32), identity=ident[:])
+        b0_cols = consts.tile([P, CHUNKS_0 * SETS], BF16)
+        nc.scalar.copy(out=b0_cols[:].bitcast(F32), in_=b0_bank[:, 0:CHUNKS_0])
+
+        x_codes = keep.tile([P, P], U32, align_bytes=64)
+        x_scales = keep.tile([P, P], U8, align_bytes=64)
+        w_codes = keep.tile([P, CHUNKS, SETS * P], U32, align_bytes=64)
+        w_scales = keep.tile([P, CHUNKS, SETS * P], U8, align_bytes=64)
+        h_codes = keep.tile([P, PASSES_1, P], U32, align_bytes=64)
+        h_scales = keep.tile([P, PASSES_1, P], U8, align_bytes=64)
+        h_grouped = keep.tile([P, PASSES_1, P, PACK], BF16, align_bytes=64)
+        out_sb = keep.tile([P, D2], F32)
+
+        def flip(rows, sets):
+            words = rows[:].bitcast(F32)
+            bank = flip_psum.tile([P, D2], F32, tag="bank")
+            for block in range(sets * HALVES):
+                cols = slice(block * P, (block + 1) * P)
+                nc.tensor.transpose(out=bank[:, cols], in_=words[:, cols], identity=ident[:])
+            grouped = stream.tile([P, sets * P * PACK], BF16, name="grouped", align_bytes=64)
+            nc.scalar.copy(
+                out=grouped[:].bitcast(F32).rearrange("q (s n h) -> q s n h", s=sets, h=HALVES),
+                in_=bank[:, 0 : sets * HALVES * P].rearrange(
+                    "q (s h n) -> q s n h", s=sets, h=HALVES
+                ),
+            )
+            return grouped
+
+        x_grouped = flip(x_rows, 1)
+        nc.vector.quantize_mx(
+            out=x_codes[:].bitcast(FP8X4), scales=x_scales[:], in_=x_grouped[:]
+        )
+
+        grouped_of = {}
+        out_banks = {}
+
+        def front(c):
+            masked = stream.tile([P, CHUNK], BF16, name="masked")
+            nc.vector.tensor_mul(out=masked[:], in0=w_rows[c][:], in1=m_rows[c][:])
+            grouped_of[c] = flip(masked, SETS)
+
+        def quantise(c):
+            nc.vector.quantize_mx(
+                out=w_codes[:, c, :].bitcast(FP8X4),
+                scales=w_scales[:, c, :],
+                in_=grouped_of[c][:],
+            )
+
+        def multiply(c):
+            if c < CHUNKS_0:
+                h_bank = h_psum.tile([P, SETS, P], F32)
+                for e in range(SETS):
+                    cols = slice(e * P, (e + 1) * P)
+                    nc.tensor.matmul_mx(
+                        out=h_bank[:, e, :],
+                        lhsT=w_codes[:, c, cols].bitcast(FP8X4),
+                        lhsT_scale=w_scales[:, c, cols],
+                        rhs=x_codes[:].bitcast(FP8X4),
+                        rhs_scale=x_scales[:],
+                        start=True,
+                        stop=True,
+                    )
+                for e in range(SETS):
+                    pas, t = divmod(SETS * c + e, PACK)
+                    nc.scalar.activation(
+                        out=h_grouped[:, pas, :, t],
+                        in_=h_bank[:, e, :],
+                        func=RELU,
+                        bias=b0_cols[:, SETS * c + e : SETS * c + e + 1],
+                    )
+            else:
+                out_banks[c] = out_psum.tile([P, P], F32, name="out_bank")
+                for pas in range(PASSES_1):
+                    cols = slice(pas * P, (pas + 1) * P)
+                    nc.tensor.matmul_mx(
+                        out=out_banks[c][:],
+                        lhsT=h_codes[:, pas, :].bitcast(FP8X4),
+                        lhsT_scale=h_scales[:, pas, :],
+                        rhs=w_codes[:, c, cols].bitcast(FP8X4),
+                        rhs_scale=w_scales[:, c, cols],
+                        start=(pas == 0),
+                        stop=(pas == PASSES_1 - 1),
+                    )
+
+        def back(c):
+            if c < CHUNKS_0:
+                pas, half = divmod(c, HALVES)
+                if half == HALVES - 1:
+                    nc.vector.quantize_mx(
+                        out=h_codes[:, pas, :].bitcast(FP8X4),
+                        scales=h_scales[:, pas, :],
+                        in_=h_grouped[:, pas, :, :].rearrange("q b t -> q (b t)"),
+                    )
+            else:
+                cols = slice((c - CHUNKS_0) * P, (c - CHUNKS_0 + 1) * P)
+                nc.vector.tensor_add(out=out_sb[:, cols], in0=out_banks[c][:], in1=b1_all[:, cols])
+                nc.vector.tensor_scalar_max(out=out_sb[:, cols], in0=out_sb[:, cols], scalar1=0.0)
+                nc.sync.dma_start(out=out[:, cols], in_=out_sb[:, cols])
+
+        for i in range(CHUNKS + 2):
+            if i < CHUNKS:
+                front(i)
+            if 0 <= i - 1 < CHUNKS:
+                quantise(i - 1)
+            if 0 <= i - 2:
+                back(i - 2)
+            if 0 <= i - 1 < CHUNKS:
+                multiply(i - 1)

@@ -35,6 +35,14 @@ def tile_patchedsparsenetwork_pa_s_kernel(tc, x, W0, b0, m0, W1, b1, m1, out):
         h_psum = ctx.enter_context(tc.psum_pool(name="h_psum", bufs=2))
         out_psum = ctx.enter_context(tc.psum_pool(name="out_psum", bufs=2))
 
+        b1_rows = consts.tile([P, D2], BF16)
+        nc.vector.memset(b1_rows[:], 0.0)
+        nc.scalar.dma_start(out=b1_rows[0:1, :], in_=b1.rearrange("(o n) -> o n", o=1))
+        b0_rows = consts.tile([P, HALVES * P], BF16)
+        nc.vector.memset(b0_rows[:], 0.0)
+        nc.scalar.dma_start(
+            out=b0_rows[0:CHUNKS_0, :], in_=b0.rearrange("(j n) -> j n", j=CHUNKS_0)
+        )
         x_rows = consts.tile([P, D0], BF16)
         nc.sync.dma_start(out=x_rows[:], in_=x)
         w_views = [W0.rearrange("(c q e) k -> c q (e k)", q=P, e=SETS)[c] for c in range(CHUNKS_0)]
@@ -53,19 +61,11 @@ def tile_patchedsparsenetwork_pa_s_kernel(tc, x, W0, b0, m0, W1, b1, m1, out):
         ones = consts.tile([P, P], BF16)
         nc.vector.memset(ones[:], 1.0)
 
-        b1_rows = consts.tile([P, D2], BF16)
-        nc.vector.memset(b1_rows[:], 0.0)
-        nc.scalar.dma_start(out=b1_rows[0:1, :], in_=b1.rearrange("(o n) -> o n", o=1))
         b1_bank = flip_psum.tile([P, D2], F32, tag="bank")
         nc.tensor.matmul(out=b1_bank[:], lhsT=ones[:], rhs=b1_rows[:], start=True, stop=True)
         b1_all = consts.tile([P, D2], F32)
         nc.scalar.copy(out=b1_all[:], in_=b1_bank[:])
 
-        b0_rows = consts.tile([P, HALVES * P], BF16)
-        nc.vector.memset(b0_rows[:], 0.0)
-        nc.scalar.dma_start(
-            out=b0_rows[0:CHUNKS_0, :], in_=b0.rearrange("(j n) -> j n", j=CHUNKS_0)
-        )
         b0_bank = flip_psum.tile([P, D2], F32, tag="bank")
         nc.tensor.transpose(out=b0_bank[:, 0:P], in_=b0_rows[:].bitcast(F32), identity=ident[:])
         b0_cols = consts.tile([P, CHUNKS_0 * SETS], BF16)

@@ -23,28 +23,29 @@ CHUNKS_0 = D1 * D0 // (P * CHUNK)
 CHUNKS_1 = D2 * D1 // (P * CHUNK)
 CHUNKS = CHUNKS_0 + CHUNKS_1
 PASSES_1 = D1 // K_PASS
+LAG = 2
 
 
 def tile_patchedsparsenetwork_pa_s_kernel(tc, x, W0, b0, m0, W1, b1, m1, out):
     nc = tc.nc
     with ExitStack() as ctx:
+        ctx.enter_context(tc.manual_schedule())
         consts = ctx.enter_context(tc.tile_pool(name="consts", bufs=1))
         keep = ctx.enter_context(tc.tile_pool(name="keep", bufs=1))
         stream = ctx.enter_context(tc.tile_pool(name="stream", bufs=CHUNKS))
         flip_psum = ctx.enter_context(tc.psum_pool(name="flip_psum", bufs=4))
-        h_psum = ctx.enter_context(tc.psum_pool(name="h_psum", bufs=2))
-        out_psum = ctx.enter_context(tc.psum_pool(name="out_psum", bufs=2))
+        sum_psum = ctx.enter_context(tc.psum_pool(name="sum_psum", bufs=4))
 
-        b1_rows = consts.tile([P, D2], BF16)
-        nc.vector.memset(b1_rows[:], 0.0)
-        nc.scalar.dma_start(out=b1_rows[0:1, :], in_=b1.rearrange("(o n) -> o n", o=1))
-        b0_rows = consts.tile([P, HALVES * P], BF16)
-        nc.vector.memset(b0_rows[:], 0.0)
-        nc.scalar.dma_start(
-            out=b0_rows[0:CHUNKS_0, :], in_=b0.rearrange("(j n) -> j n", j=CHUNKS_0)
-        )
         x_rows = consts.tile([P, D0], BF16)
         nc.sync.dma_start(out=x_rows[:], in_=x)
+        b0_rows = consts.tile([P, HALVES * P], BF16)
+        nc.vector.memset(b0_rows[:], 0.0)
+        nc.sync.dma_start(
+            out=b0_rows[0:CHUNKS_0, :], in_=b0.rearrange("(j n) -> j n", j=CHUNKS_0)
+        )
+        b1_rows = consts.tile([P, D2], BF16)
+        nc.vector.memset(b1_rows[:], 0.0)
+        nc.sync.dma_start(out=b1_rows[0:1, :], in_=b1.rearrange("(o n) -> o n", o=1))
         w_views = [W0.rearrange("(c q e) k -> c q (e k)", q=P, e=SETS)[c] for c in range(CHUNKS_0)]
         m_views = [m0.rearrange("(c q e) k -> c q (e k)", q=P, e=SETS)[c] for c in range(CHUNKS_0)]
         w_views += [W1.rearrange("(r q) k -> r q k", q=P)[r] for r in range(CHUNKS_1)]
@@ -61,22 +62,13 @@ def tile_patchedsparsenetwork_pa_s_kernel(tc, x, W0, b0, m0, W1, b1, m1, out):
         ones = consts.tile([P, P], BF16)
         nc.vector.memset(ones[:], 1.0)
 
-        b1_bank = flip_psum.tile([P, D2], F32, tag="bank")
-        nc.tensor.matmul(out=b1_bank[:], lhsT=ones[:], rhs=b1_rows[:], start=True, stop=True)
-        b1_all = consts.tile([P, D2], F32)
-        nc.scalar.copy(out=b1_all[:], in_=b1_bank[:])
-
-        b0_bank = flip_psum.tile([P, D2], F32, tag="bank")
-        nc.tensor.transpose(out=b0_bank[:, 0:P], in_=b0_rows[:].bitcast(F32), identity=ident[:])
-        b0_cols = consts.tile([P, CHUNKS_0 * SETS], BF16)
-        nc.scalar.copy(out=b0_cols[:].bitcast(F32), in_=b0_bank[:, 0:CHUNKS_0])
-
         x_codes = keep.tile([P, P], U32, align_bytes=64)
         x_scales = keep.tile([P, P], U8, align_bytes=64)
         w_codes = keep.tile([P, CHUNKS, SETS * P], U32, align_bytes=64)
         w_scales = keep.tile([P, CHUNKS, SETS * P], U8, align_bytes=64)
         h_codes = keep.tile([P, PASSES_1, P], U32, align_bytes=64)
         h_scales = keep.tile([P, PASSES_1, P], U8, align_bytes=64)
+        h_tiles = keep.tile([P, PASSES_1, PACK, P], BF16)
         h_grouped = keep.tile([P, PASSES_1, P, PACK], BF16, align_bytes=64)
         out_sb = keep.tile([P, D2], F32)
 
@@ -96,9 +88,16 @@ def tile_patchedsparsenetwork_pa_s_kernel(tc, x, W0, b0, m0, W1, b1, m1, out):
             return grouped
 
         x_grouped = flip(x_rows, 1)
-        nc.vector.quantize_mx(
-            out=x_codes[:].bitcast(FP8X4), scales=x_scales[:], in_=x_grouped[:]
-        )
+
+        b0_bank = flip_psum.tile([P, D2], F32, tag="bank")
+        nc.tensor.transpose(out=b0_bank[:, 0:P], in_=b0_rows[:].bitcast(F32), identity=ident[:])
+        b0_cols = consts.tile([P, CHUNKS_0 * SETS], BF16)
+        nc.scalar.copy(out=b0_cols[:].bitcast(F32), in_=b0_bank[:, 0:CHUNKS_0])
+
+        b1_bank = flip_psum.tile([P, D2], F32, tag="bank")
+        nc.tensor.matmul(out=b1_bank[:], lhsT=ones[:], rhs=b1_rows[:], start=True, stop=True)
+        b1_all = consts.tile([P, D2], F32)
+        nc.scalar.copy(out=b1_all[:], in_=b1_bank[:])
 
         grouped_of = {}
         out_banks = {}
@@ -115,63 +114,81 @@ def tile_patchedsparsenetwork_pa_s_kernel(tc, x, W0, b0, m0, W1, b1, m1, out):
                 in_=grouped_of[c][:],
             )
 
-        def multiply(c):
-            if c < CHUNKS_0:
-                h_bank = h_psum.tile([P, SETS, P], F32)
-                for e in range(SETS):
-                    cols = slice(e * P, (e + 1) * P)
-                    nc.tensor.matmul_mx(
-                        out=h_bank[:, e, :],
-                        lhsT=w_codes[:, c, cols].bitcast(FP8X4),
-                        lhsT_scale=w_scales[:, c, cols],
-                        rhs=x_codes[:].bitcast(FP8X4),
-                        rhs_scale=x_scales[:],
-                        start=True,
-                        stop=True,
-                    )
-                for e in range(SETS):
-                    pas, t = divmod(SETS * c + e, PACK)
-                    nc.scalar.activation(
-                        out=h_grouped[:, pas, :, t],
-                        in_=h_bank[:, e, :],
-                        func=RELU,
-                        bias=b0_cols[:, SETS * c + e : SETS * c + e + 1],
-                    )
-            else:
-                out_banks[c] = out_psum.tile([P, P], F32, name="out_bank")
-                for pas in range(PASSES_1):
-                    cols = slice(pas * P, (pas + 1) * P)
-                    nc.tensor.matmul_mx(
-                        out=out_banks[c][:],
-                        lhsT=h_codes[:, pas, :].bitcast(FP8X4),
-                        lhsT_scale=h_scales[:, pas, :],
-                        rhs=w_codes[:, c, cols].bitcast(FP8X4),
-                        rhs_scale=w_scales[:, c, cols],
-                        start=(pas == 0),
-                        stop=(pas == PASSES_1 - 1),
-                    )
+        def multiply_0(c):
+            h_bank = sum_psum.tile([P, SETS, P], F32, tag="sum")
+            for e in range(SETS):
+                cols = slice(e * P, (e + 1) * P)
+                nc.tensor.matmul_mx(
+                    out=h_bank[:, e, :],
+                    lhsT=w_codes[:, c, cols].bitcast(FP8X4),
+                    lhsT_scale=w_scales[:, c, cols],
+                    rhs=x_codes[:].bitcast(FP8X4),
+                    rhs_scale=x_scales[:],
+                    start=True,
+                    stop=True,
+                )
+            for e in range(SETS):
+                pas, t = divmod(SETS * c + e, PACK)
+                nc.scalar.activation(
+                    out=h_tiles[:, pas, t, :],
+                    in_=h_bank[:, e, :],
+                    func=RELU,
+                    bias=b0_cols[:, SETS * c + e : SETS * c + e + 1],
+                )
 
-        def back(c):
-            if c < CHUNKS_0:
-                pas, half = divmod(c, HALVES)
-                if half == HALVES - 1:
-                    nc.vector.quantize_mx(
-                        out=h_codes[:, pas, :].bitcast(FP8X4),
-                        scales=h_scales[:, pas, :],
-                        in_=h_grouped[:, pas, :, :].rearrange("q b t -> q (b t)"),
-                    )
-            else:
-                cols = slice((c - CHUNKS_0) * P, (c - CHUNKS_0 + 1) * P)
-                nc.vector.tensor_add(out=out_sb[:, cols], in0=out_banks[c][:], in1=b1_all[:, cols])
-                nc.vector.tensor_scalar_max(out=out_sb[:, cols], in0=out_sb[:, cols], scalar1=0.0)
-                nc.sync.dma_start(out=out[:, cols], in_=out_sb[:, cols])
+        def group_h(pas):
+            nc.vector.tensor_copy(
+                out=h_grouped[:, pas, :, :], in_=h_tiles[:, pas, :, :].rearrange("q t b -> q b t")
+            )
 
-        for i in range(CHUNKS + 2):
+        def quantise_h(pas):
+            nc.vector.quantize_mx(
+                out=h_codes[:, pas, :].bitcast(FP8X4),
+                scales=h_scales[:, pas, :],
+                in_=h_grouped[:, pas, :, :].rearrange("q b t -> q (b t)"),
+            )
+
+        def multiply_1(c):
+            out_banks[c] = sum_psum.tile([P, P], F32, name="out_bank", tag="sum")
+            for pas in range(PASSES_1):
+                cols = slice(pas * P, (pas + 1) * P)
+                nc.tensor.matmul_mx(
+                    out=out_banks[c][:],
+                    lhsT=h_codes[:, pas, :].bitcast(FP8X4),
+                    lhsT_scale=h_scales[:, pas, :],
+                    rhs=w_codes[:, c, cols].bitcast(FP8X4),
+                    rhs_scale=w_scales[:, c, cols],
+                    start=(pas == 0),
+                    stop=(pas == PASSES_1 - 1),
+                )
+
+        def finish_out(c):
+            cols = slice((c - CHUNKS_0) * P, (c - CHUNKS_0 + 1) * P)
+            nc.vector.tensor_add(out=out_sb[:, cols], in0=out_banks[c][:], in1=b1_all[:, cols])
+            nc.vector.tensor_scalar_max(out=out_sb[:, cols], in0=out_sb[:, cols], scalar1=0.0)
+            nc.sync.dma_start(out=out[:, cols], in_=out_sb[:, cols])
+
+        layer_0 = range(CHUNKS_0)
+        layer_1 = range(CHUNKS_0, CHUNKS)
+        h_done = CHUNKS_0 - 1 + 2 * LAG
+        multiply_step = {c: max(c + LAG, h_done) for c in layer_1}
+        for i in range(CHUNKS + 2 * LAG):
             if i < CHUNKS:
                 front(i)
-            if 0 <= i - 1 < CHUNKS:
-                quantise(i - 1)
-            if 0 <= i - 2:
-                back(i - 2)
-            if 0 <= i - 1 < CHUNKS:
-                multiply(i - 1)
+            if i == 0:
+                nc.vector.quantize_mx(
+                    out=x_codes[:].bitcast(FP8X4), scales=x_scales[:], in_=x_grouped[:]
+                )
+            for c in layer_1:
+                if i == multiply_step[c] + LAG:
+                    finish_out(c)
+            if 0 <= i - LAG < CHUNKS:
+                quantise(i - LAG)
+            if i - 2 * LAG in layer_0 and (i - 2 * LAG) % HALVES == HALVES - 1:
+                group_h((i - 2 * LAG) // HALVES)
+                quantise_h((i - 2 * LAG) // HALVES)
+            if i - LAG in layer_0:
+                multiply_0(i - LAG)
+            for c in layer_1:
+                if i == multiply_step[c]:
+                    multiply_1(c)

@@ -32,7 +32,9 @@ def tile_patchedsparsenetwork_pa_s_kernel(tc, x, W0, b0, m0, W1, b1, m1, out):
         ctx.enter_context(tc.manual_schedule())
         consts = ctx.enter_context(tc.tile_pool(name="consts", bufs=1))
         keep = ctx.enter_context(tc.tile_pool(name="keep", bufs=1))
-        stream = ctx.enter_context(tc.tile_pool(name="stream", bufs=CHUNKS))
+        pieces = {c: [(0, SETS)] for c in range(CHUNKS)}
+        pieces[CHUNKS - 1] = [(s, 1) for s in range(SETS)]
+        stream = ctx.enter_context(tc.tile_pool(name="stream", bufs=CHUNKS + 1))
         flip_psum = ctx.enter_context(tc.psum_pool(name="flip_psum", bufs=4))
         sum_psum = ctx.enter_context(tc.psum_pool(name="sum_psum", bufs=4))
 
@@ -53,9 +55,11 @@ def tile_patchedsparsenetwork_pa_s_kernel(tc, x, W0, b0, m0, W1, b1, m1, out):
         w_rows, m_rows = [], []
         for c in range(CHUNKS):
             w_rows.append(stream.tile([P, CHUNK], BF16, name="w_rows"))
-            nc.sync.dma_start(out=w_rows[c][:], in_=w_views[c])
             m_rows.append(stream.tile([P, CHUNK], BF16, name="m_rows"))
-            nc.sync.dma_start(out=m_rows[c][:], in_=m_views[c])
+            for first, sets in pieces[c]:
+                cols = slice(first * K_PASS, (first + sets) * K_PASS)
+                nc.sync.dma_start(out=w_rows[c][:, cols], in_=w_views[c][:, cols])
+                nc.sync.dma_start(out=m_rows[c][:, cols], in_=m_views[c][:, cols])
 
         ident = consts.tile([P, P], F32)
         make_identity(nc, ident[:])
@@ -73,7 +77,7 @@ def tile_patchedsparsenetwork_pa_s_kernel(tc, x, W0, b0, m0, W1, b1, m1, out):
         out_sb = keep.tile([P, D2], F32)
 
         def flip(rows, sets):
-            words = rows[:].bitcast(F32)
+            words = rows.bitcast(F32)
             bank = flip_psum.tile([P, D2], F32, tag="bank")
             for block in range(sets * HALVES):
                 cols = slice(block * P, (block + 1) * P)
@@ -87,7 +91,7 @@ def tile_patchedsparsenetwork_pa_s_kernel(tc, x, W0, b0, m0, W1, b1, m1, out):
             )
             return grouped
 
-        x_grouped = flip(x_rows, 1)
+        x_grouped = flip(x_rows[:], 1)
 
         b0_bank = flip_psum.tile([P, D2], F32, tag="bank")
         nc.tensor.transpose(out=b0_bank[:, 0:P], in_=b0_rows[:].bitcast(F32), identity=ident[:])
@@ -104,15 +108,21 @@ def tile_patchedsparsenetwork_pa_s_kernel(tc, x, W0, b0, m0, W1, b1, m1, out):
 
         def front(c):
             masked = stream.tile([P, CHUNK], BF16, name="masked")
-            nc.vector.tensor_mul(out=masked[:], in0=w_rows[c][:], in1=m_rows[c][:])
-            grouped_of[c] = flip(masked, SETS)
+            for first, sets in pieces[c]:
+                cols = slice(first * K_PASS, (first + sets) * K_PASS)
+                nc.vector.tensor_mul(
+                    out=masked[:, cols], in0=w_rows[c][:, cols], in1=m_rows[c][:, cols]
+                )
+                grouped_of[c, first] = flip(masked[:, cols], sets)
 
         def quantise(c):
-            nc.vector.quantize_mx(
-                out=w_codes[:, c, :].bitcast(FP8X4),
-                scales=w_scales[:, c, :],
-                in_=grouped_of[c][:],
-            )
+            for first, sets in pieces[c]:
+                cols = slice(first * P, (first + sets) * P)
+                nc.vector.quantize_mx(
+                    out=w_codes[:, c, cols].bitcast(FP8X4),
+                    scales=w_scales[:, c, cols],
+                    in_=grouped_of[c, first][:],
+                )
 
         def multiply_0(c):
             h_bank = sum_psum.tile([P, SETS, P], F32, tag="sum")
@@ -179,14 +189,14 @@ def tile_patchedsparsenetwork_pa_s_kernel(tc, x, W0, b0, m0, W1, b1, m1, out):
                 nc.vector.quantize_mx(
                     out=x_codes[:].bitcast(FP8X4), scales=x_scales[:], in_=x_grouped[:]
                 )
-            for c in layer_1:
-                if i == multiply_step[c] + LAG:
-                    finish_out(c)
             if 0 <= i - LAG < CHUNKS:
                 quantise(i - LAG)
             if i - 2 * LAG in layer_0 and (i - 2 * LAG) % HALVES == HALVES - 1:
                 group_h((i - 2 * LAG) // HALVES)
                 quantise_h((i - 2 * LAG) // HALVES)
+            for c in layer_1:
+                if i == multiply_step[c] + LAG:
+                    finish_out(c)
             if i - LAG in layer_0:
                 multiply_0(i - LAG)
             for c in layer_1:

@@ -72,7 +72,6 @@ def tile_patchedsparsenetwork_pa_s_kernel(tc, x, W0, b0, m0, W1, b1, m1, out):
         w_scales = keep.tile([P, CHUNKS, SETS * P], U8, align_bytes=64)
         h_codes = keep.tile([P, PASSES_1, P], U32, align_bytes=64)
         h_scales = keep.tile([P, PASSES_1, P], U8, align_bytes=64)
-        h_tiles = keep.tile([P, PASSES_1, PACK, P], BF16)
         h_grouped = keep.tile([P, PASSES_1, P, PACK], BF16, align_bytes=64)
         out_sb = keep.tile([P, D2], F32)
 
@@ -140,16 +139,11 @@ def tile_patchedsparsenetwork_pa_s_kernel(tc, x, W0, b0, m0, W1, b1, m1, out):
             for e in range(SETS):
                 pas, t = divmod(SETS * c + e, PACK)
                 nc.scalar.activation(
-                    out=h_tiles[:, pas, t, :],
+                    out=h_grouped[:, pas, :, t],
                     in_=h_bank[:, e, :],
                     func=RELU,
                     bias=b0_cols[:, SETS * c + e : SETS * c + e + 1],
                 )
-
-        def group_h(pas):
-            nc.vector.tensor_copy(
-                out=h_grouped[:, pas, :, :], in_=h_tiles[:, pas, :, :].rearrange("q t b -> q b t")
-            )
 
         def quantise_h(pas):
             nc.vector.quantize_mx(
@@ -192,7 +186,6 @@ def tile_patchedsparsenetwork_pa_s_kernel(tc, x, W0, b0, m0, W1, b1, m1, out):
             if 0 <= i - LAG < CHUNKS:
                 quantise(i - LAG)
             if i - 2 * LAG in layer_0 and (i - 2 * LAG) % HALVES == HALVES - 1:
-                group_h((i - 2 * LAG) // HALVES)
                 quantise_h((i - 2 * LAG) // HALVES)
             for c in layer_1:
                 if i == multiply_step[c] + LAG:

from contextlib import ExitStack

import concourse.mybir as mybir
from concourse.masks import make_identity

BF16 = mybir.dt.bfloat16
F32 = mybir.dt.float32
U32 = mybir.dt.uint32
U8 = mybir.dt.uint8
FP8X4 = mybir.dt.float8_e4m3fn_x4
RELU = mybir.ActivationFunctionType.Relu

P = 128
PACK = 4
K_PASS = P * PACK
HALVES = 2
D0, D1, D2 = 512, 1024, 512
FLOPS = 2 * P * (D0 * D1 + D1 * D2)

SETS = 2
CHUNK = SETS * K_PASS
CHUNKS_0 = D1 * D0 // (P * CHUNK)
CHUNKS_1 = D2 * D1 // (P * CHUNK)
CHUNKS = CHUNKS_0 + CHUNKS_1
PASSES_1 = D1 // K_PASS
LAG = 2


def tile_patchedsparsenetwork_pa_s_kernel(tc, x, W0, b0, m0, W1, b1, m1, out):
    nc = tc.nc
    with ExitStack() as ctx:
        ctx.enter_context(tc.manual_schedule())
        consts = ctx.enter_context(tc.tile_pool(name="consts", bufs=1))
        keep = ctx.enter_context(tc.tile_pool(name="keep", bufs=1))
        pieces = {c: [(0, SETS)] for c in range(CHUNKS)}
        pieces[CHUNKS - 1] = [(s, 1) for s in range(SETS)]
        stream = ctx.enter_context(tc.tile_pool(name="stream", bufs=CHUNKS + 1))
        flip_psum = ctx.enter_context(tc.psum_pool(name="flip_psum", bufs=4))
        sum_psum = ctx.enter_context(tc.psum_pool(name="sum_psum", bufs=4))

        x_rows = consts.tile([P, D0], BF16)
        nc.sync.dma_start(out=x_rows[:], in_=x)
        b0_rows = consts.tile([P, HALVES * P], BF16)
        nc.vector.memset(b0_rows[:], 0.0)
        nc.sync.dma_start(
            out=b0_rows[0:CHUNKS_0, :], in_=b0.rearrange("(j n) -> j n", j=CHUNKS_0)
        )
        b1_rows = consts.tile([P, D2], BF16)
        nc.vector.memset(b1_rows[:], 0.0)
        nc.sync.dma_start(out=b1_rows[0:1, :], in_=b1.rearrange("(o n) -> o n", o=1))
        w_views = [W0.rearrange("(c q e) k -> c q (e k)", q=P, e=SETS)[c] for c in range(CHUNKS_0)]
        m_views = [m0.rearrange("(c q e) k -> c q (e k)", q=P, e=SETS)[c] for c in range(CHUNKS_0)]
        w_views += [W1.rearrange("(r q) k -> r q k", q=P)[r] for r in range(CHUNKS_1)]
        m_views += [m1.rearrange("(r q) k -> r q k", q=P)[r] for r in range(CHUNKS_1)]
        w_rows, m_rows = [], []
        for c in range(CHUNKS):
            w_rows.append(stream.tile([P, CHUNK], BF16, name="w_rows"))
            m_rows.append(stream.tile([P, CHUNK], BF16, name="m_rows"))
            for first, sets in pieces[c]:
                cols = slice(first * K_PASS, (first + sets) * K_PASS)
                nc.sync.dma_start(out=w_rows[c][:, cols], in_=w_views[c][:, cols])
                nc.sync.dma_start(out=m_rows[c][:, cols], in_=m_views[c][:, cols])

        ident = consts.tile([P, P], F32)
        make_identity(nc, ident[:])
        ones = consts.tile([P, P], BF16)
        nc.vector.memset(ones[:], 1.0)

        x_codes = keep.tile([P, P], U32, align_bytes=64)
        x_scales = keep.tile([P, P], U8, align_bytes=64)
        w_codes = keep.tile([P, CHUNKS, SETS * P], U32, align_bytes=64)
        w_scales = keep.tile([P, CHUNKS, SETS * P], U8, align_bytes=64)
        h_codes = keep.tile([P, PASSES_1, P], U32, align_bytes=64)
        h_scales = keep.tile([P, PASSES_1, P], U8, align_bytes=64)
        h_grouped = keep.tile([P, PASSES_1, P, PACK], BF16, align_bytes=64)
        out_sb = keep.tile([P, D2], F32)

        def flip(rows, sets):
            words = rows.bitcast(F32)
            bank = flip_psum.tile([P, D2], F32, tag="bank")
            for block in range(sets * HALVES):
                cols = slice(block * P, (block + 1) * P)
                nc.tensor.transpose(out=bank[:, cols], in_=words[:, cols], identity=ident[:])
            grouped = stream.tile([P, sets * P * PACK], BF16, name="grouped", align_bytes=64)
            nc.scalar.copy(
                out=grouped[:].bitcast(F32).rearrange("q (s n h) -> q s n h", s=sets, h=HALVES),
                in_=bank[:, 0 : sets * HALVES * P].rearrange(
                    "q (s h n) -> q s n h", s=sets, h=HALVES
                ),
            )
            return grouped

        x_grouped = flip(x_rows[:], 1)

        b0_bank = flip_psum.tile([P, D2], F32, tag="bank")
        nc.tensor.transpose(out=b0_bank[:, 0:P], in_=b0_rows[:].bitcast(F32), identity=ident[:])
        b0_cols = consts.tile([P, CHUNKS_0 * SETS], BF16)
        nc.scalar.copy(out=b0_cols[:].bitcast(F32), in_=b0_bank[:, 0:CHUNKS_0])

        b1_bank = flip_psum.tile([P, D2], F32, tag="bank")
        nc.tensor.matmul(out=b1_bank[:], lhsT=ones[:], rhs=b1_rows[:], start=True, stop=True)
        b1_all = consts.tile([P, D2], F32)
        nc.scalar.copy(out=b1_all[:], in_=b1_bank[:])

        grouped_of = {}
        out_banks = {}

        def front(c):
            masked = stream.tile([P, CHUNK], BF16, name="masked")
            for first, sets in pieces[c]:
                cols = slice(first * K_PASS, (first + sets) * K_PASS)
                nc.vector.tensor_mul(
                    out=masked[:, cols], in0=w_rows[c][:, cols], in1=m_rows[c][:, cols]
                )
                grouped_of[c, first] = flip(masked[:, cols], sets)

        def quantise(c):
            for first, sets in pieces[c]:
                cols = slice(first * P, (first + sets) * P)
                nc.vector.quantize_mx(
                    out=w_codes[:, c, cols].bitcast(FP8X4),
                    scales=w_scales[:, c, cols],
                    in_=grouped_of[c, first][:],
                )

        def multiply_0(c):
            h_bank = sum_psum.tile([P, SETS, P], F32, tag="sum")
            for e in range(SETS):
                cols = slice(e * P, (e + 1) * P)
                nc.tensor.matmul_mx(
                    out=h_bank[:, e, :],
                    lhsT=w_codes[:, c, cols].bitcast(FP8X4),
                    lhsT_scale=w_scales[:, c, cols],
                    rhs=x_codes[:].bitcast(FP8X4),
                    rhs_scale=x_scales[:],
                    start=True,
                    stop=True,
                )
            for e in range(SETS):
                pas, t = divmod(SETS * c + e, PACK)
                nc.scalar.activation(
                    out=h_grouped[:, pas, :, t],
                    in_=h_bank[:, e, :],
                    func=RELU,
                    bias=b0_cols[:, SETS * c + e : SETS * c + e + 1],
                )

        def quantise_h(pas):
            nc.vector.quantize_mx(
                out=h_codes[:, pas, :].bitcast(FP8X4),
                scales=h_scales[:, pas, :],
                in_=h_grouped[:, pas, :, :].rearrange("q b t -> q (b t)"),
            )

        def multiply_1(c):
            out_banks[c] = sum_psum.tile([P, P], F32, name="out_bank", tag="sum")
            for pas in range(PASSES_1):
                cols = slice(pas * P, (pas + 1) * P)
                nc.tensor.matmul_mx(
                    out=out_banks[c][:],
                    lhsT=h_codes[:, pas, :].bitcast(FP8X4),
                    lhsT_scale=h_scales[:, pas, :],
                    rhs=w_codes[:, c, cols].bitcast(FP8X4),
                    rhs_scale=w_scales[:, c, cols],
                    start=(pas == 0),
                    stop=(pas == PASSES_1 - 1),
                )

        def finish_out(c):
            cols = slice((c - CHUNKS_0) * P, (c - CHUNKS_0 + 1) * P)
            nc.vector.tensor_add(out=out_sb[:, cols], in0=out_banks[c][:], in1=b1_all[:, cols])
            nc.vector.tensor_scalar_max(out=out_sb[:, cols], in0=out_sb[:, cols], scalar1=0.0)
            nc.sync.dma_start(out=out[:, cols], in_=out_sb[:, cols])

        layer_0 = range(CHUNKS_0)
        layer_1 = range(CHUNKS_0, CHUNKS)
        h_done = CHUNKS_0 - 1 + 2 * LAG
        multiply_step = {c: max(c + LAG, h_done) for c in layer_1}
        for i in range(CHUNKS + 2 * LAG):
            if i < CHUNKS:
                front(i)
            if i == 0:
                nc.vector.quantize_mx(
                    out=x_codes[:].bitcast(FP8X4), scales=x_scales[:], in_=x_grouped[:]
                )
            if 0 <= i - LAG < CHUNKS:
                quantise(i - LAG)
            if i - 2 * LAG in layer_0 and (i - 2 * LAG) % HALVES == HALVES - 1:
                quantise_h((i - 2 * LAG) // HALVES)
            for c in layer_1:
                if i == multiply_step[c] + LAG:
                    finish_out(c)
            if i - LAG in layer_0:
                multiply_0(i - LAG)
            for c in layer_1:
                if i == multiply_step[c]:
                    multiply_1(c)
